import numpy as np
import ml_dtypes


def mxq(x, axis, fmt="e4m3"):
    dtype, down = {"e4m3": (ml_dtypes.float8_e4m3fn, 7), "e5m2": (ml_dtypes.float8_e5m2, 14)}[fmt]
    v = np.moveaxis(np.asarray(x, np.float32).astype(ml_dtypes.bfloat16).astype(np.float64), axis, -1)
    blocks = v.reshape(v.shape[:-1] + (-1, 32))
    amax = np.abs(blocks).max(-1, keepdims=True)
    byte = np.maximum(np.where(amax > 0, np.frexp(amax)[1] - 1 + 127, 0) - down, 1)
    scale = np.exp2(byte - 127.0)
    codes = (blocks / scale).astype(np.float32).astype(dtype).astype(np.float64)
    return np.moveaxis((codes * scale).reshape(v.shape), -1, axis)


WIDE = False


def mx_kscale(k):
    if not WIDE:
        return np.ones(k)
    levels = np.array([10, -10, 5, -5, 0])
    if k % 512:
        return np.exp2(np.random.permutation(np.resize(levels, k // 32))).repeat(32)
    a = np.empty((k // 512, 16))
    for p in range(k // 512):
        a[p, :8] = np.random.permutation(np.resize(levels, 8))
        for g in range(8):
            far = levels[np.abs(levels - a[p, g]) >= 10]
            a[p, g + 8] = far[np.random.randint(len(far))]
    return np.exp2(a.ravel()).repeat(32)


BF16 = ml_dtypes.bfloat16


def bf(x):
    return np.asarray(x, np.float32).astype(BF16)


def f64(x):
    return np.asarray(x).astype(np.float64)


B, C, HH, WW, NH, HD, F = 4, 512, 16, 16, 8, 64, 2048
EPS = 1e-5


def layer_norm(v, w, b):
    mu = v.mean(-1, keepdims=True)
    var = ((v - mu) ** 2).mean(-1, keepdims=True)
    return (v - mu) * (1.0 / np.sqrt(var + EPS)) * w + b


def draw0():
    s = mx_kscale(F)
    return {"h": bf(np.maximum(np.random.standard_normal((B, HH, WW, F)), 0.0) * 0.125 * s),
            "ffn2_w": bf(np.random.standard_normal((C, F)) * 0.5 / np.sqrt(F) / s),
            "ffn2_b": bf(np.random.standard_normal(C) * 0.02),
            "scale_ffn": bf(0.1 * (1.0 + 0.1 * np.random.standard_normal(1))),
            "ln2_w": bf(1.0 + 0.1 * np.random.standard_normal(C)),
            "ln2_b": bf(0.1 * np.random.standard_normal(C)),
            "scale_norm2": bf(1.5 * (1.0 + 0.1 * np.random.standard_normal(1))),
            "x": bf(np.random.standard_normal((B, C, HH, WW)))}


def core(h, ffn2_w, ffn2_b, scale_ffn, ln2_w, ln2_b, scale_norm2, x):
    y2 = ((mxq(f64(h), 3, "e4m3") @ mxq(f64(ffn2_w), 1, "e4m3").T) + f64(ffn2_b)) * f64(scale_ffn)
    y2 = layer_norm(y2, f64(ln2_w), f64(ln2_b)) * f64(scale_norm2)
    out = np.maximum(y2 + f64(x).transpose(0, 2, 3, 1), 0.0)
    return out.transpose(0, 3, 1, 2)


def e4m3fn_bytes(y):
    return np.clip(np.asarray(y, np.float64), -448.0, 448.0).astype(np.float32).astype(ml_dtypes.float8_e4m3fn).view(np.uint8)


def e4m3fn_values(b):
    return np.asarray(b, np.uint8).view(ml_dtypes.float8_e4m3fn).astype(np.float64)


def setup_inputs():
    d = draw0()
    x0 = np.asarray(d['h']).astype(np.float64)
    s = (np.max(np.abs(x0), axis=(0, 1, 2), keepdims=True) / 448.0).astype(np.float32)
    out = {}
    for k, v in d.items():
        if k == 'h':
            out['h_bytes'] = e4m3fn_bytes(x0 / s.astype(np.float64))
            out['h_scale'] = s
        else:
            out[k] = v
    return out


def reference(h_bytes, h_scale, ffn2_w, ffn2_b, scale_ffn, ln2_w, ln2_b, scale_norm2, x):
    return core(e4m3fn_values(h_bytes) * h_scale.astype(np.float64), ffn2_w, ffn2_b, scale_ffn, ln2_w, ln2_b, scale_norm2, x)

@@ -1,0 +1,303 @@
+from contextlib import ExitStack
+
+import concourse.mybir as mybir
+from concourse.masks import make_identity
+
+F32 = mybir.dt.float32
+BF16 = mybir.dt.bfloat16
+U32 = mybir.dt.uint32
+U8 = mybir.dt.uint8
+FP8 = mybir.dt.float8_e4m3fn
+FP8X4 = mybir.dt.float8_e4m3fn_x4
+ALU = mybir.AluOpType
+ACT = mybir.ActivationFunctionType
+
+P = 128
+PIX = 1024
+NT = PIX // P
+K = 2048
+G = K // 512
+C = 512
+J = C // P
+HW = 256
+EPS = 1e-5
+
+FLOPS = 2 * PIX * K * C
+
+
+def tile_transformerconvblock_pc_kernel(
+    tc, h_bytes, h_scale, ffn2_w, ffn2_b, scale_ffn, ln2_w, ln2_b, scale_norm2, x, out
+):
+    nc = tc.nc
+    h_rows = h_bytes.rearrange("b i j k -> (b i j) k")
+    hs_rows = h_scale.rearrange("a b c (m n) -> (a b c m) n", n=P)
+
+    with ExitStack() as ctx:
+        const = ctx.enter_context(tc.tile_pool(name="const", bufs=1))
+        work = ctx.enter_context(tc.tile_pool(name="work", bufs=4))
+        stat = ctx.enter_context(tc.tile_pool(name="stat", bufs=4))
+        psum = ctx.enter_context(tc.psum_pool(name="psum", bufs=2))
+
+        ident = const.tile([P, P], F32, name="ident")
+        make_identity(nc, ident[:])
+
+        srow = const.tile([P, P], F32, name="srow")
+        nc.sync.dma_start(out=srow[0:16, :], in_=hs_rows)
+        nc.sync.dma_start(out=srow[16:32, :], in_=hs_rows)
+        nc.vector.memset(srow[32:64, :], 0.0)
+        nc.vector.memset(srow[64:128, :], 0.0)
+
+        hby = []
+        for i in range(NT):
+            hby_i = const.tile([P, K], U8, name="hby%d" % i)
+            hby.append(hby_i)
+        wraw = []
+        for j in range(J):
+            wraw_j = const.tile([P, K], BF16, name="wraw%d" % j)
+            wraw.append(wraw_j)
+
+        def load_h(i):
+            nc.sync.dma_start(out=hby[i][:], in_=h_rows[P * i : P * (i + 1), :])
+
+        def load_w(j):
+            nc.sync.dma_start(out=wraw[j][:], in_=ffn2_w[P * j : P * (j + 1), :])
+
+        load_h(0)
+        load_w(0)
+        load_h(1)
+        load_w(1)
+        load_w(2)
+        load_h(2)
+        load_w(3)
+        load_h(3)
+        vraw = const.tile([P, P], BF16, name="vraw")
+        nc.gpsimd.memset(vraw[:], 0.0)
+        nc.sync.dma_start(out=vraw[0:J, :], in_=ln2_w.rearrange("(j p) -> j p", p=P))
+        nc.sync.dma_start(out=vraw[J : 2 * J, :], in_=ln2_b.rearrange("(j p) -> j p", p=P))
+        nc.sync.dma_start(out=vraw[2 * J : 3 * J, :], in_=ffn2_b.rearrange("(j p) -> j p", p=P))
+        nc.sync.dma_start(out=vraw[12:13, 0:1], in_=scale_ffn.rearrange("(a b) -> a b", a=1))
+        nc.sync.dma_start(out=vraw[12:13, 16:17], in_=scale_norm2.rearrange("(a b) -> a b", a=1))
+
+
+        x_sb = const.tile([P, 4, J, HW], BF16, name="x_sb")
+
+        def load_x(b):
+            nc.sync.dma_start(
+                out=x_sb[:, b, :, :], in_=x[b].rearrange("(j p) h w -> p j (h w)", p=P)
+            )
+
+        load_h(4)
+        load_h(5)
+        load_x(0)
+        load_h(6)
+        load_h(7)
+        load_x(1)
+        load_x(2)
+        load_x(3)
+
+        one = const.tile([P, 1], F32, name="one")
+        nc.vector.memset(one[:], 1.0)
+        warm = const.tile([P, 1], F32, name="warm")
+        nc.scalar.activation(out=warm[:], in_=one[:], func=ACT.Abs_reciprocal_sqrt)
+
+        def spread(dst, col):
+            nc.tensor.transpose(dst, col.to_broadcast([P, P]), ident[:])
+
+        sT = psum.tile([P, 512], F32, tag="tr", bufs=4, name="sT")
+        nc.tensor.transpose(sT[:, 0:P], srow[:], ident[:])
+        scol = const.tile([P, 16], F32, name="scol")
+        nc.vector.tensor_copy(out=scol[:], in_=sT[:, 0:16])
+        sc = const.tile([P, K], F32, name="sc")
+        for q in range(4):
+            sb = psum.tile([P, 512], F32, tag="tr", bufs=4, name="sb")
+            for m in range(4):
+                spread(sb[:, P * m : P * (m + 1)], scol[:, 4 * q + m : 4 * q + m + 1])
+            if q == 0:
+                nc.vector.tensor_copy(out=sc[:, 0:512], in_=sb[:])
+            else:
+                nc.scalar.copy(out=sc[:, 512 * q : 512 * (q + 1)], in_=sb[:])
+
+        wg = const.tile([P, G * C * 4], BF16, name="wg", align_bytes=64)
+        wc = const.tile([P, G * C], U32, name="wc", align_bytes=64)
+        wsc = const.tile([P, G * C], U8, name="wsc", align_bytes=64)
+        wgw = wg[:].bitcast(F32).rearrange("p (g c u) -> p g c u", g=G, u=2)
+
+        def turn(words, hf, dst):
+            tr = psum.tile([P, 512], F32, tag="tr", bufs=4, name="tr")
+            for gg in range(2):
+                g = 2 * hf + gg
+                for u in range(2):
+                    nc.tensor.transpose(
+                        tr[:, (2 * gg + u) * P : (2 * gg + u + 1) * P],
+                        words[:, 256 * g + u : 256 * (g + 1) : 2],
+                        ident[:],
+                    )
+            nc.scalar.copy(out=dst, in_=tr[:].rearrange("p (g u r) -> p g r u", g=2, u=2))
+
+        def w_turn(j):
+            words = wraw[j][:].bitcast(F32)
+            for hf in range(2):
+                turn(words, hf, wgw[:, 2 * hf : 2 * hf + 2, P * j : P * (j + 1), :])
+
+        def w_quant():
+            for g in range(G):
+                nc.vector.quantize_mx(
+                    out=wc[:, C * g : C * (g + 1)].bitcast(FP8X4),
+                    scales=wsc[:, C * g : C * (g + 1)],
+                    in_=wg[:, 4 * C * g : 4 * C * (g + 1)],
+                )
+
+        hcs = {}
+
+        def front(i):
+            hb = work.tile([P, K], BF16, name="hb")
+            nchunk = 4 if i == 0 else 2
+            wdt = K // nchunk
+            for q in range(nchunk):
+                cs = slice(wdt * q, wdt * (q + 1))
+                nc.vector.tensor_tensor(
+                    out=hb[:, cs], in0=hby[i][:, cs].bitcast(FP8), in1=sc[:, cs], op=ALU.mult
+                )
+            words = hb[:].bitcast(F32)
+            hg = work.tile([P, K], BF16, name="hg", align_bytes=64)
+            hgw = hg[:].bitcast(F32).rearrange("p (g r u) -> p g r u", g=G, u=2)
+            for hf in range(2):
+                turn(words, hf, hgw[:, 2 * hf : 2 * hf + 2, :, :])
+            hc = work.tile([P, K // 4], U32, name="hc", align_bytes=64)
+            hs = work.tile([P, K // 4], U8, name="hs", align_bytes=64)
+            nc.vector.quantize_mx(out=hc[:].bitcast(FP8X4), scales=hs[:], in_=hg[:])
+            hcs[i] = (hc, hs)
+
+        nrms = {}
+        nts = {}
+        cst = {}
+
+        def small_vectors():
+            vf = const.tile([P, P], F32, name="vf")
+            nc.scalar.copy(out=vf[:], in_=vraw[:])
+            vT = psum.tile([P, 512], F32, tag="tr", bufs=4, name="vT")
+            nc.tensor.transpose(vT[:, 0:P], vf[:], ident[:])
+            vcol = const.tile([P, 16], F32, name="vcol")
+            nc.scalar.copy(out=vcol[:], in_=vT[:, 0:16])
+            cst["vT"] = vT
+            cst["vcol"] = vcol
+
+        def small_vectors_2():
+            vT = cst["vT"]
+            vcol = cst["vcol"]
+            spread(vT[:, P : 2 * P], vcol[:, 12:13])
+            sv = const.tile([P, 17], F32, name="sv")
+            nc.scalar.copy(out=sv[:], in_=vT[:, P : P + 17])
+            bT = psum.tile([P, 512], F32, tag="tr", bufs=4, name="bT")
+            for j in range(J):
+                spread(bT[:, P * j : P * (j + 1)], vcol[:, 2 * J + j : 2 * J + j + 1])
+            bias_t = const.tile([P, C], F32, name="bias_t")
+            nc.scalar.copy(out=bias_t[:], in_=bT[:])
+            c1 = const.tile([P, 1], F32, name="c1")
+            nc.gpsimd.tensor_scalar(
+                out=c1[:], in0=sv[:, 0:1], scalar1=sv[:, 0:1], scalar2=1.0 / C,
+                op0=ALU.mult, op1=ALU.mult,
+            )
+            sn = const.tile([P, 1], F32, name="sn")
+            nc.gpsimd.tensor_scalar(
+                out=sn[:], in0=sv[:, 0:1], scalar1=sv[:, 16:17], scalar2=1.0,
+                op0=ALU.mult, op1=ALU.mult,
+            )
+            gain = const.tile([P, J], F32, name="gain")
+            nc.gpsimd.tensor_scalar(
+                out=gain[:], in0=vcol[:, 0:J], scalar1=sn[:, 0:1], scalar2=1.0,
+                op0=ALU.mult, op1=ALU.mult,
+            )
+            beta = const.tile([P, J], F32, name="beta")
+            nc.gpsimd.tensor_scalar(
+                out=beta[:], in0=vcol[:, J : 2 * J], scalar1=sv[:, 16:17], scalar2=1.0,
+                op0=ALU.mult, op1=ALU.mult,
+            )
+            cst["bias"] = bias_t
+            cst["c1"] = c1
+            cst["gain"] = gain
+            cst["beta"] = beta
+
+        def mx_norm(i):
+            hc, hs = hcs[i]
+            acc = psum.tile([P, C], F32, tag="acc", bufs=2, name="acc")
+            for g in range(G):
+                nc.tensor.matmul_mx(
+                    out=acc[:],
+                    lhsT=hc[:, P * g : P * (g + 1)].bitcast(FP8X4),
+                    lhsT_scale=hs[:, P * g : P * (g + 1)],
+                    rhs=wc[:, C * g : C * (g + 1)].bitcast(FP8X4),
+                    rhs_scale=wsc[:, C * g : C * (g + 1)],
+                    start=(g == 0),
+                    stop=(g == G - 1),
+                )
+            v = work.tile([P, C], F32, name="v")
+            vsum = stat.tile([P, 1], F32, name="vsum")
+            nc.vector.scalar_tensor_tensor(
+                out=v[:], in0=acc[:], scalar=1.0, in1=cst["bias"][:], op0=ALU.mult, op1=ALU.add,
+                accum_out=vsum[:],
+            )
+            nmean = stat.tile([P, 1], F32, name="nmean")
+            nc.scalar.activation(out=nmean[:], in_=vsum[:], func=ACT.Copy, scale=-1.0 / C)
+            junk = work.tile([P, C], F32, name="junk")
+            ssq = stat.tile([P, 1], F32, name="ssq")
+            nc.scalar.activation(
+                out=junk[:], in_=v[:], func=ACT.Square, bias=nmean[:, 0:1], scale=1.0,
+                accum_out=ssq[:],
+            )
+            rs = stat.tile([P, 1], F32, name="rs")
+            nc.scalar.activation(
+                out=rs[:], in_=ssq[:], func=ACT.Abs_reciprocal_sqrt, bias=EPS,
+                scale=cst["c1"][:, 0:1],
+            )
+            nmr = stat.tile([P, 1], F32, name="nmr")
+            nc.scalar.activation(out=nmr[:], in_=nmean[:], func=ACT.Copy, scale=rs[:, 0:1])
+            nrm = work.tile([P, C], F32, name="nrm")
+            nc.scalar.activation(
+                out=nrm[:], in_=v[:], func=ACT.Identity, bias=nmr[:, 0:1], scale=rs[:, 0:1]
+            )
+            nrms[i] = nrm
+
+        def finish(i):
+            b, half = i // 2, i % 2
+            nrm = nrms[i]
+            if half == 0:
+                nt0 = psum.tile([P, 2, HW], F32, tag="nt", bufs=2, name="nt0")
+                nt1 = psum.tile([P, 2, HW], F32, tag="nt", bufs=2, name="nt1")
+                nts[b] = (nt0, nt1)
+            for j in range(J):
+                nc.tensor.transpose(
+                    nts[b][j // 2][:, j % 2, P * half : P * (half + 1)],
+                    nrm[:, P * j : P * (j + 1)],
+                    ident[:],
+                )
+            if half == 1:
+                out_b = out[b].rearrange("(j p) h w -> p j (h w)", p=P)
+                for j in range(J):
+                    sx = work.tile([P, HW], F32, name="sx")
+                    nc.vector.scalar_tensor_tensor(
+                        out=sx[:], in0=nts[b][j // 2][:, j % 2, :], scalar=cst["gain"][:, j : j + 1],
+                        in1=x_sb[:, b, j, :], op0=ALU.mult, op1=ALU.add,
+                    )
+                    o = work.tile([P, HW], F32, name="o")
+                    nc.scalar.activation(
+                        out=o[:], in_=sx[:], func=ACT.Relu, bias=cst["beta"][:, j : j + 1], scale=1.0
+                    )
+                    nc.sync.dma_start(out=out_b[:, j, :], in_=o[:])
+
+        w_turn(0)
+        front(0)
+        w_turn(1)
+        w_turn(2)
+        front(1)
+        w_turn(3)
+        w_quant()
+        small_vectors()
+        small_vectors_2()
+        for i in range(NT):
+            if i + 2 < NT:
+                front(i + 2)
+            mx_norm(i)
+            if i >= 1:
+                finish(i - 1)
+        finish(NT - 1)

@@ -253,9 +253,15 @@ def tile_transformerconvblock_pc_kernel(
             nmr = stat.tile([P, 1], F32, name="nmr")
             nc.scalar.activation(out=nmr[:], in_=nmean[:], func=ACT.Copy, scale=rs[:, 0:1])
             nrm = work.tile([P, C], F32, name="nrm")
-            nc.scalar.activation(
-                out=nrm[:], in_=v[:], func=ACT.Identity, bias=nmr[:, 0:1], scale=rs[:, 0:1]
-            )
+            if i >= NT - 2:
+                nc.vector.tensor_scalar(
+                    out=nrm[:], in0=v[:], scalar1=rs[:, 0:1], scalar2=nmr[:, 0:1],
+                    op0=ALU.mult, op1=ALU.add,
+                )
+            else:
+                nc.scalar.activation(
+                    out=nrm[:], in_=v[:], func=ACT.Identity, bias=nmr[:, 0:1], scale=rs[:, 0:1]
+                )
             nrms[i] = nrm
 
         def finish(i):
@@ -280,9 +286,15 @@ def tile_transformerconvblock_pc_kernel(
                         in1=x_sb[:, b, j, :], op0=ALU.mult, op1=ALU.add,
                     )
                     o = work.tile([P, HW], F32, name="o")
-                    nc.scalar.activation(
-                        out=o[:], in_=sx[:], func=ACT.Relu, bias=cst["beta"][:, j : j + 1], scale=1.0
-                    )
+                    if b == 3 and j % 2 == 1:
+                        nc.vector.tensor_scalar(
+                            out=o[:], in0=sx[:], scalar1=cst["beta"][:, j : j + 1], scalar2=0.0,
+                            op0=ALU.add, op1=ALU.max,
+                        )
+                    else:
+                        nc.scalar.activation(
+                            out=o[:], in_=sx[:], func=ACT.Relu, bias=cst["beta"][:, j : j + 1], scale=1.0
+                        )
                     nc.sync.dma_start(out=out_b[:, j, :], in_=o[:])
 
         w_turn(0)

@@ -41,6 +41,12 @@ def tile_transformerconvblock_pc_kernel(
         ident = const.tile([P, P], F32, name="ident")
         make_identity(nc, ident[:])
 
+        zb = const.tile([P, 512], BF16, name="zb")
+        nc.vector.memset(zb[:], 0.0)
+        dm = psum.tile([P, 512], F32, tag="acc", bufs=2, name="dm")
+        for r in range(4):
+            nc.tensor.matmul(out=dm[:], lhsT=zb[:, 0:P], rhs=zb[:], start=True, stop=True)
+
         srow = const.tile([P, P], F32, name="srow")
         nc.sync.dma_start(out=srow[0:16, :], in_=hs_rows)
         nc.sync.dma_start(out=srow[16:32, :], in_=hs_rows)

@@ -259,7 +259,7 @@ def tile_transformerconvblock_pc_kernel(
             nmr = stat.tile([P, 1], F32, name="nmr")
             nc.scalar.activation(out=nmr[:], in_=nmean[:], func=ACT.Copy, scale=rs[:, 0:1])
             nrm = work.tile([P, C], F32, name="nrm")
-            if i >= NT - 2:
+            if i >= NT - 4:
                 nc.vector.tensor_scalar(
                     out=nrm[:], in0=v[:], scalar1=rs[:, 0:1], scalar2=nmr[:, 0:1],
                     op0=ALU.mult, op1=ALU.add,

from contextlib import ExitStack

import concourse.mybir as mybir
from concourse.masks import make_identity

F32 = mybir.dt.float32
BF16 = mybir.dt.bfloat16
U32 = mybir.dt.uint32
U8 = mybir.dt.uint8
FP8 = mybir.dt.float8_e4m3fn
FP8X4 = mybir.dt.float8_e4m3fn_x4
ALU = mybir.AluOpType
ACT = mybir.ActivationFunctionType

P = 128
PIX = 1024
NT = PIX // P
K = 2048
G = K // 512
C = 512
J = C // P
HW = 256
EPS = 1e-5

FLOPS = 2 * PIX * K * C


def tile_transformerconvblock_pc_kernel(
    tc, h_bytes, h_scale, ffn2_w, ffn2_b, scale_ffn, ln2_w, ln2_b, scale_norm2, x, out
):
    nc = tc.nc
    h_rows = h_bytes.rearrange("b i j k -> (b i j) k")
    hs_rows = h_scale.rearrange("a b c (m n) -> (a b c m) n", n=P)

    with ExitStack() as ctx:
        const = ctx.enter_context(tc.tile_pool(name="const", bufs=1))
        work = ctx.enter_context(tc.tile_pool(name="work", bufs=4))
        stat = ctx.enter_context(tc.tile_pool(name="stat", bufs=4))
        psum = ctx.enter_context(tc.psum_pool(name="psum", bufs=2))

        ident = const.tile([P, P], F32, name="ident")
        make_identity(nc, ident[:])

        zb = const.tile([P, 512], BF16, name="zb")
        nc.vector.memset(zb[:], 0.0)
        dm = psum.tile([P, 512], F32, tag="acc", bufs=2, name="dm")
        for r in range(4):
            nc.tensor.matmul(out=dm[:], lhsT=zb[:, 0:P], rhs=zb[:], start=True, stop=True)

        srow = const.tile([P, P], F32, name="srow")
        nc.sync.dma_start(out=srow[0:16, :], in_=hs_rows)
        nc.sync.dma_start(out=srow[16:32, :], in_=hs_rows)
        nc.vector.memset(srow[32:64, :], 0.0)
        nc.vector.memset(srow[64:128, :], 0.0)

        hby = []
        for i in range(NT):
            hby_i = const.tile([P, K], U8, name="hby%d" % i)
            hby.append(hby_i)
        wraw = []
        for j in range(J):
            wraw_j = const.tile([P, K], BF16, name="wraw%d" % j)
            wraw.append(wraw_j)

        def load_h(i):
            nc.sync.dma_start(out=hby[i][:], in_=h_rows[P * i : P * (i + 1), :])

        def load_w(j):
            nc.sync.dma_start(out=wraw[j][:], in_=ffn2_w[P * j : P * (j + 1), :])

        load_h(0)
        load_w(0)
        load_h(1)
        load_w(1)
        load_w(2)
        load_h(2)
        load_w(3)
        load_h(3)
        vraw = const.tile([P, P], BF16, name="vraw")
        nc.gpsimd.memset(vraw[:], 0.0)
        nc.sync.dma_start(out=vraw[0:J, :], in_=ln2_w.rearrange("(j p) -> j p", p=P))
        nc.sync.dma_start(out=vraw[J : 2 * J, :], in_=ln2_b.rearrange("(j p) -> j p", p=P))
        nc.sync.dma_start(out=vraw[2 * J : 3 * J, :], in_=ffn2_b.rearrange("(j p) -> j p", p=P))
        nc.sync.dma_start(out=vraw[12:13, 0:1], in_=scale_ffn.rearrange("(a b) -> a b", a=1))
        nc.sync.dma_start(out=vraw[12:13, 16:17], in_=scale_norm2.rearrange("(a b) -> a b", a=1))


        x_sb = const.tile([P, 4, J, HW], BF16, name="x_sb")

        def load_x(b):
            nc.sync.dma_start(
                out=x_sb[:, b, :, :], in_=x[b].rearrange("(j p) h w -> p j (h w)", p=P)
            )

        load_h(4)
        load_h(5)
        load_x(0)
        load_h(6)
        load_h(7)
        load_x(1)
        load_x(2)
        load_x(3)

        one = const.tile([P, 1], F32, name="one")
        nc.vector.memset(one[:], 1.0)
        warm = const.tile([P, 1], F32, name="warm")
        nc.scalar.activation(out=warm[:], in_=one[:], func=ACT.Abs_reciprocal_sqrt)

        def spread(dst, col):
            nc.tensor.transpose(dst, col.to_broadcast([P, P]), ident[:])

        sT = psum.tile([P, 512], F32, tag="tr", bufs=4, name="sT")
        nc.tensor.transpose(sT[:, 0:P], srow[:], ident[:])
        scol = const.tile([P, 16], F32, name="scol")
        nc.vector.tensor_copy(out=scol[:], in_=sT[:, 0:16])
        sc = const.tile([P, K], F32, name="sc")
        for q in range(4):
            sb = psum.tile([P, 512], F32, tag="tr", bufs=4, name="sb")
            for m in range(4):
                spread(sb[:, P * m : P * (m + 1)], scol[:, 4 * q + m : 4 * q + m + 1])
            if q == 0:
                nc.vector.tensor_copy(out=sc[:, 0:512], in_=sb[:])
            else:
                nc.scalar.copy(out=sc[:, 512 * q : 512 * (q + 1)], in_=sb[:])

        wg = const.tile([P, G * C * 4], BF16, name="wg", align_bytes=64)
        wc = const.tile([P, G * C], U32, name="wc", align_bytes=64)
        wsc = const.tile([P, G * C], U8, name="wsc", align_bytes=64)
        wgw = wg[:].bitcast(F32).rearrange("p (g c u) -> p g c u", g=G, u=2)

        def turn(words, hf, dst):
            tr = psum.tile([P, 512], F32, tag="tr", bufs=4, name="tr")
            for gg in range(2):
                g = 2 * hf + gg
                for u in range(2):
                    nc.tensor.transpose(
                        tr[:, (2 * gg + u) * P : (2 * gg + u + 1) * P],
                        words[:, 256 * g + u : 256 * (g + 1) : 2],
                        ident[:],
                    )
            nc.scalar.copy(out=dst, in_=tr[:].rearrange("p (g u r) -> p g r u", g=2, u=2))

        def w_turn(j):
            words = wraw[j][:].bitcast(F32)
            for hf in range(2):
                turn(words, hf, wgw[:, 2 * hf : 2 * hf + 2, P * j : P * (j + 1), :])

        def w_quant():
            for g in range(G):
                nc.vector.quantize_mx(
                    out=wc[:, C * g : C * (g + 1)].bitcast(FP8X4),
                    scales=wsc[:, C * g : C * (g + 1)],
                    in_=wg[:, 4 * C * g : 4 * C * (g + 1)],
                )

        hcs = {}

        def front(i):
            hb = work.tile([P, K], BF16, name="hb")
            nchunk = 4 if i == 0 else 2
            wdt = K // nchunk
            for q in range(nchunk):
                cs = slice(wdt * q, wdt * (q + 1))
                nc.vector.tensor_tensor(
                    out=hb[:, cs], in0=hby[i][:, cs].bitcast(FP8), in1=sc[:, cs], op=ALU.mult
                )
            words = hb[:].bitcast(F32)
            hg = work.tile([P, K], BF16, name="hg", align_bytes=64)
            hgw = hg[:].bitcast(F32).rearrange("p (g r u) -> p g r u", g=G, u=2)
            for hf in range(2):
                turn(words, hf, hgw[:, 2 * hf : 2 * hf + 2, :, :])
            hc = work.tile([P, K // 4], U32, name="hc", align_bytes=64)
            hs = work.tile([P, K // 4], U8, name="hs", align_bytes=64)
            nc.vector.quantize_mx(out=hc[:].bitcast(FP8X4), scales=hs[:], in_=hg[:])
            hcs[i] = (hc, hs)

        nrms = {}
        nts = {}
        cst = {}

        def small_vectors():
            vf = const.tile([P, P], F32, name="vf")
            nc.scalar.copy(out=vf[:], in_=vraw[:])
            vT = psum.tile([P, 512], F32, tag="tr", bufs=4, name="vT")
            nc.tensor.transpose(vT[:, 0:P], vf[:], ident[:])
            vcol = const.tile([P, 16], F32, name="vcol")
            nc.scalar.copy(out=vcol[:], in_=vT[:, 0:16])
            cst["vT"] = vT
            cst["vcol"] = vcol

        def small_vectors_2():
            vT = cst["vT"]
            vcol = cst["vcol"]
            spread(vT[:, P : 2 * P], vcol[:, 12:13])
            sv = const.tile([P, 17], F32, name="sv")
            nc.scalar.copy(out=sv[:], in_=vT[:, P : P + 17])
            bT = psum.tile([P, 512], F32, tag="tr", bufs=4, name="bT")
            for j in range(J):
                spread(bT[:, P * j : P * (j + 1)], vcol[:, 2 * J + j : 2 * J + j + 1])
            bias_t = const.tile([P, C], F32, name="bias_t")
            nc.scalar.copy(out=bias_t[:], in_=bT[:])
            c1 = const.tile([P, 1], F32, name="c1")
            nc.gpsimd.tensor_scalar(
                out=c1[:], in0=sv[:, 0:1], scalar1=sv[:, 0:1], scalar2=1.0 / C,
                op0=ALU.mult, op1=ALU.mult,
            )
            sn = const.tile([P, 1], F32, name="sn")
            nc.gpsimd.tensor_scalar(
                out=sn[:], in0=sv[:, 0:1], scalar1=sv[:, 16:17], scalar2=1.0,
                op0=ALU.mult, op1=ALU.mult,
            )
            gain = const.tile([P, J], F32, name="gain")
            nc.gpsimd.tensor_scalar(
                out=gain[:], in0=vcol[:, 0:J], scalar1=sn[:, 0:1], scalar2=1.0,
                op0=ALU.mult, op1=ALU.mult,
            )
            beta = const.tile([P, J], F32, name="beta")
            nc.gpsimd.tensor_scalar(
                out=beta[:], in0=vcol[:, J : 2 * J], scalar1=sv[:, 16:17], scalar2=1.0,
                op0=ALU.mult, op1=ALU.mult,
            )
            cst["bias"] = bias_t
            cst["c1"] = c1
            cst["gain"] = gain
            cst["beta"] = beta

        def mx_norm(i):
            hc, hs = hcs[i]
            acc = psum.tile([P, C], F32, tag="acc", bufs=2, name="acc")
            for g in range(G):
                nc.tensor.matmul_mx(
                    out=acc[:],
                    lhsT=hc[:, P * g : P * (g + 1)].bitcast(FP8X4),
                    lhsT_scale=hs[:, P * g : P * (g + 1)],
                    rhs=wc[:, C * g : C * (g + 1)].bitcast(FP8X4),
                    rhs_scale=wsc[:, C * g : C * (g + 1)],
                    start=(g == 0),
                    stop=(g == G - 1),
                )
            v = work.tile([P, C], F32, name="v")
            vsum = stat.tile([P, 1], F32, name="vsum")
            nc.vector.scalar_tensor_tensor(
                out=v[:], in0=acc[:], scalar=1.0, in1=cst["bias"][:], op0=ALU.mult, op1=ALU.add,
                accum_out=vsum[:],
            )
            nmean = stat.tile([P, 1], F32, name="nmean")
            nc.scalar.activation(out=nmean[:], in_=vsum[:], func=ACT.Copy, scale=-1.0 / C)
            junk = work.tile([P, C], F32, name="junk")
            ssq = stat.tile([P, 1], F32, name="ssq")
            nc.scalar.activation(
                out=junk[:], in_=v[:], func=ACT.Square, bias=nmean[:, 0:1], scale=1.0,
                accum_out=ssq[:],
            )
            rs = stat.tile([P, 1], F32, name="rs")
            nc.scalar.activation(
                out=rs[:], in_=ssq[:], func=ACT.Abs_reciprocal_sqrt, bias=EPS,
                scale=cst["c1"][:, 0:1],
            )
            nmr = stat.tile([P, 1], F32, name="nmr")
            nc.scalar.activation(out=nmr[:], in_=nmean[:], func=ACT.Copy, scale=rs[:, 0:1])
            nrm = work.tile([P, C], F32, name="nrm")
            if i >= NT - 4:
                nc.vector.tensor_scalar(
                    out=nrm[:], in0=v[:], scalar1=rs[:, 0:1], scalar2=nmr[:, 0:1],
                    op0=ALU.mult, op1=ALU.add,
                )
            else:
                nc.scalar.activation(
                    out=nrm[:], in_=v[:], func=ACT.Identity, bias=nmr[:, 0:1], scale=rs[:, 0:1]
                )
            nrms[i] = nrm

        def finish(i):
            b, half = i // 2, i % 2
            nrm = nrms[i]
            if half == 0:
                nt0 = psum.tile([P, 2, HW], F32, tag="nt", bufs=2, name="nt0")
                nt1 = psum.tile([P, 2, HW], F32, tag="nt", bufs=2, name="nt1")
                nts[b] = (nt0, nt1)
            for j in range(J):
                nc.tensor.transpose(
                    nts[b][j // 2][:, j % 2, P * half : P * (half + 1)],
                    nrm[:, P * j : P * (j + 1)],
                    ident[:],
                )
            if half == 1:
                out_b = out[b].rearrange("(j p) h w -> p j (h w)", p=P)
                for j in range(J):
                    sx = work.tile([P, HW], F32, name="sx")
                    nc.vector.scalar_tensor_tensor(
                        out=sx[:], in0=nts[b][j // 2][:, j % 2, :], scalar=cst["gain"][:, j : j + 1],
                        in1=x_sb[:, b, j, :], op0=ALU.mult, op1=ALU.add,
                    )
                    o = work.tile([P, HW], F32, name="o")
                    if b == 3 and j % 2 == 1:
                        nc.vector.tensor_scalar(
                            out=o[:], in0=sx[:], scalar1=cst["beta"][:, j : j + 1], scalar2=0.0,
                            op0=ALU.add, op1=ALU.max,
                        )
                    else:
                        nc.scalar.activation(
                            out=o[:], in_=sx[:], func=ACT.Relu, bias=cst["beta"][:, j : j + 1], scale=1.0
                        )
                    nc.sync.dma_start(out=out_b[:, j, :], in_=o[:])

        w_turn(0)
        front(0)
        w_turn(1)
        w_turn(2)
        front(1)
        w_turn(3)
        w_quant()
        small_vectors()
        small_vectors_2()
        for i in range(NT):
            if i + 2 < NT:
                front(i + 2)
            mx_norm(i)
            if i >= 1:
                finish(i - 1)
        finish(NT - 1)
